import numpy as np
import ml_dtypes


def mxq(x, axis, fmt="e4m3"):
    dtype, down = {"e4m3": (ml_dtypes.float8_e4m3fn, 7), "e5m2": (ml_dtypes.float8_e5m2, 14)}[fmt]
    v = np.moveaxis(np.asarray(x, np.float32).astype(ml_dtypes.bfloat16).astype(np.float64), axis, -1)
    blocks = v.reshape(v.shape[:-1] + (-1, 32))
    amax = np.abs(blocks).max(-1, keepdims=True)
    byte = np.maximum(np.where(amax > 0, np.frexp(amax)[1] - 1 + 127, 0) - down, 1)
    scale = np.exp2(byte - 127.0)
    codes = (blocks / scale).astype(np.float32).astype(dtype).astype(np.float64)
    return np.moveaxis((codes * scale).reshape(v.shape), -1, axis)


WIDE = False


def mx_kscale(k):
    if not WIDE:
        return np.ones(k)
    levels = np.array([10, -10, 5, -5, 0])
    if k % 512:
        return np.exp2(np.random.permutation(np.resize(levels, k // 32))).repeat(32)
    a = np.empty((k // 512, 16))
    for p in range(k // 512):
        a[p, :8] = np.random.permutation(np.resize(levels, 8))
        for g in range(8):
            far = levels[np.abs(levels - a[p, g]) >= 10]
            a[p, g + 8] = far[np.random.randint(len(far))]
    return np.exp2(a.ravel()).repeat(32)


BF16 = ml_dtypes.bfloat16


def bf(x):
    return np.asarray(x, np.float32).astype(BF16)


def f64(x):
    return np.asarray(x).astype(np.float64)


B, S, H, NH, NKV, HD = 2, 256, 2048, 16, 4, 128
ROPE_THETA = 10000.0


def rope_tables():
    inv_freq = 1.0 / (ROPE_THETA ** (np.arange(0, HD, 2) / HD))
    pos = np.arange(S)[None, :] + np.random.randint(0, S, (B, 1))
    freqs = pos[:, :, None] * inv_freq[None, None, :]
    emb = np.concatenate([freqs, freqs], axis=-1)
    return np.cos(emb), np.sin(emb)


def rotate_half(x):
    x1, x2 = np.split(x, 2, axis=-1)
    return np.concatenate([-x2, x1], axis=-1)


def setup_inputs():
    s = mx_kscale(H)
    hidden_states = bf(np.random.standard_normal((B, S, H)) * s)
    q_w = bf(np.random.standard_normal((NH * HD, H)) / np.sqrt(H) / s[None, :])
    k_w = bf(np.random.standard_normal((NKV * HD, H)) / np.sqrt(H) / s[None, :])
    v_w = bf(np.random.standard_normal((NKV * HD, H)) / np.sqrt(H) / s[None, :])
    cos, sin = rope_tables()
    return {"hidden_states": hidden_states, "cos": bf(cos), "sin": bf(sin), "q_w": q_w, "k_w": k_w, "v_w": v_w}


def reference(hidden_states, cos, sin, q_w, k_w, v_w):
    b, s, _ = hidden_states.shape
    xq = mxq(f64(hidden_states), 2, "e4m3")
    q = (xq @ mxq(f64(q_w), 1, "e4m3").T).reshape(b, s, NH, HD).transpose(0, 2, 1, 3)
    k = (xq @ mxq(f64(k_w), 1, "e4m3").T).reshape(b, s, NKV, HD).transpose(0, 2, 1, 3)
    v = (xq @ mxq(f64(v_w), 1, "e4m3").T).reshape(b, s, NKV, HD).transpose(0, 2, 1, 3)
    c = f64(cos)[:, None, :, :]
    sn = f64(sin)[:, None, :, :]
    q = q * c + rotate_half(q) * sn
    k = k * c + rotate_half(k) * sn
    return (q, k, v)

@@ -1,0 +1,298 @@
+from contextlib import ExitStack
+
+import concourse.mybir as mybir
+from concourse.masks import make_identity
+
+FLOPS = 2 * 512 * 3072 * 2048
+
+BF16 = mybir.dt.bfloat16
+F32 = mybir.dt.float32
+U32 = mybir.dt.uint32
+U8 = mybir.dt.uint8
+FP8X4 = mybir.dt.float8_e4m3fn_x4
+MULT = mybir.AluOpType.mult
+ADD = mybir.AluOpType.add
+
+P = 128
+LOAD_ORDER = (0, 2, 1, 3, 4, 5, 6, 7, 8, 9, 10, 11, 12, 13)
+HALVED = (0, 1, 2, 3)
+VECTOR_ADDS = (2, 11)
+FIRST_V_UNIT = 12
+
+
+def tile_mistralattention_kernel(
+    tc, hidden_states, cos, sin, q_w, k_w, v_w, out_0, out_1, out_2
+):
+    nc = tc.nc
+    with ExitStack() as ctx:
+        src_pool = ctx.enter_context(tc.tile_pool(name="src", bufs=1))
+        const_pool = ctx.enter_context(tc.tile_pool(name="const", bufs=1))
+        grp_pool = ctx.enter_context(tc.tile_pool(name="grp", bufs=3))
+        xq_pool = ctx.enter_context(tc.tile_pool(name="xq", bufs=1))
+        wq_pool = ctx.enter_context(tc.tile_pool(name="wq", bufs=3))
+        tt_pool = ctx.enter_context(tc.tile_pool(name="tt", bufs=3))
+        out_pool = ctx.enter_context(tc.tile_pool(name="outp", bufs=7))
+        tp_pool = ctx.enter_context(tc.psum_pool(name="tp", bufs=4))
+        acc_pool = ctx.enter_context(tc.psum_pool(name="acc", bufs=4))
+        ctx.enter_context(tc.manual_schedule())
+
+        def unit_rows(h):
+            if h < 2:
+                return hidden_states[h].rearrange("(p e) k -> p e k", e=2)
+            w = h - 2
+            if w < 8:
+                rows = q_w[256 * w : 256 * w + 256, :]
+            elif w < 10:
+                rows = k_w[256 * (w - 8) : 256 * (w - 8) + 256, :]
+            else:
+                rows = v_w[256 * (w - 10) : 256 * (w - 10) + 256, :]
+            return rows.rearrange("(r p) k -> p r k", p=P)
+
+        def unit_out(h, b):
+            w = h - 2
+            if w < 8:
+                dst = out_0[b, 2 * w : 2 * w + 2]
+            elif w < 10:
+                dst = out_1[b, 2 * (w - 8) : 2 * (w - 8) + 2]
+            else:
+                dst = out_2[b, 2 * (w - 10) : 2 * (w - 10) + 2]
+            return dst.rearrange("h (p e) d -> p h (e d)", e=2)
+
+        ident = const_pool.tile([P, P], F32, name="ident")
+        make_identity(nc, ident[:])
+        cos_sb = const_pool.tile([P, 512], BF16, name="cos_sb")
+        sin_sb = const_pool.tile([P, 512], BF16, name="sin_sb")
+
+        src = {}
+        for h in LOAD_ORDER:
+            rows = unit_rows(h)
+            if h in HALVED:
+                for i in range(2):
+                    s_t = src_pool.tile([P, 2048], BF16, name="src%d_%d" % (h, i))
+                    src[(h, i)] = s_t
+                    nc.sync.dma_start(
+                        out=s_t[:].rearrange("p (r k) -> p r k", r=2),
+                        in_=rows[:, :, 1024 * i : 1024 * i + 1024],
+                    )
+            else:
+                s_t = src_pool.tile([P, 4096], BF16, name="src%d" % h)
+                src[(h, 0)] = s_t
+                nc.sync.dma_start(out=s_t[:].rearrange("p (r k) -> p r k", r=2), in_=rows)
+            if h == 3:
+                nc.sync.dma_start(
+                    out=cos_sb[:].rearrange("p (b x) -> p b x", b=2),
+                    in_=cos.rearrange("b (p e) d -> p b (e d)", e=2),
+                )
+                nc.sync.dma_start(
+                    out=sin_sb[:].rearrange("p (b x) -> p b x", b=2),
+                    in_=sin.rearrange("b (p e) d -> p b (e d)", e=2),
+                )
+
+        def src_words(h, g, u, r):
+            if h in HALVED:
+                s_f = src[(h, g // 2)][:].bitcast(F32)
+                col = 512 * r + 256 * (g % 2)
+            else:
+                s_f = src[(h, 0)][:].bitcast(F32)
+                col = 1024 * r + 256 * g
+            return s_f[:, col + u : col + 256 : 2]
+
+        tab = const_pool.tile([P, 2048], F32, name="tab")
+        tab_w = tab[:].rearrange("p (a t h c j) -> p a t h c j", a=2, t=4, h=2, c=2)
+        tab_r = tab[:].rearrange("p (a b q c j) -> p a b q c j", a=2, b=2, q=4, c=2)
+        cos_v = cos_sb[:].rearrange("p (t f j) -> p t f j", t=4, f=2)
+        sin_v = sin_sb[:].rearrange("p (t f j) -> p t f j", t=4, f=2)
+
+        def build_tables():
+            for eng, a, c, view, f, sign in (
+                (nc.vector, 0, 0, cos_v, 0, 1.0),
+                (nc.gpsimd, 0, 1, sin_v, 1, 1.0),
+                (nc.vector, 1, 0, cos_v, 1, 1.0),
+                (nc.gpsimd, 1, 1, sin_v, 0, -1.0),
+            ):
+                eng.tensor_scalar(
+                    out=tab_w[:, a, :, :, c, :],
+                    in0=view[:, :, f, :].unsqueeze(2).to_broadcast([P, 4, 2, 64]),
+                    scalar1=sign,
+                    scalar2=0.0,
+                    op0=MULT,
+                    op1=ADD,
+                )
+
+        grouped = {}
+        codes = {}
+        planes = {}
+        banks = {}
+        sums = {}
+
+        def transposes(h, gs):
+            if h not in grouped:
+                grouped[h] = grp_pool.tile([P, 4096], BF16, name="grp", align_bytes=64)
+            for g in gs:
+                pt = tp_pool.tile([P, 512], F32, name="pt")
+                banks[(h, g)] = pt
+                for u in range(2):
+                    for r in range(2):
+                        nc.tensor.transpose(
+                            pt[:, 256 * u + 128 * r : 256 * u + 128 * r + 128],
+                            src_words(h, g, u, r),
+                            ident[:],
+                        )
+
+        def evacuate(h, gs, vector_gs):
+            g_f = grouped[h][:].bitcast(F32)
+            for g in gs:
+                dst = g_f[:, 512 * g : 512 * g + 512].rearrange("p (o u) -> p o u", u=2)
+                view = banks[(h, g)][:].rearrange("p (u o) -> p o u", u=2)
+                if g in vector_gs:
+                    nc.vector.tensor_copy(out=dst, in_=view)
+                else:
+                    nc.scalar.copy(out=dst, in_=view)
+
+        def quantise(h, parts):
+            if h not in codes:
+                pool = xq_pool if h < 2 else wq_pool
+                tag = "x%d" % h if h < 2 else "w"
+                codes[h] = pool.tile([P, 1024], U32, name="codes_" + tag, align_bytes=64)
+                planes[h] = pool.tile([P, 1024], U8, name="plane_" + tag, align_bytes=64)
+            for lo, hi in parts:
+                nc.vector.quantize_mx(
+                    out=codes[h][:, lo:hi].bitcast(FP8X4),
+                    scales=planes[h][:, lo:hi],
+                    in_=grouped[h][:, 4 * lo : 4 * hi],
+                )
+
+        WHOLE = ((0, 1024),)
+
+        def head_half(h, i):
+            gs = (2 * i, 2 * i + 1)
+            transposes(h, gs)
+            evacuate(h, gs, (2 * i + 1,))
+            quantise(h, ((512 * i, 512 * i + 512),))
+
+        def multiply(h, bs):
+            for b in bs:
+                acc = acc_pool.tile([P, 512], F32, name="acc")
+                sums[(h, b)] = acc
+                for e in range(2):
+                    for g in range(4):
+                        xs = slice(256 * g + 128 * e, 256 * g + 128 * e + 128)
+                        ws = slice(256 * g, 256 * g + 256)
+                        nc.tensor.matmul_mx(
+                            out=acc[:, 256 * e : 256 * e + 256],
+                            lhsT=codes[b][:, xs].bitcast(FP8X4),
+                            lhsT_scale=planes[b][:, xs],
+                            rhs=codes[h][:, ws].bitcast(FP8X4),
+                            rhs_scale=planes[h][:, ws],
+                            start=(g == 0),
+                            stop=(g == 3),
+                        )
+
+        results = {}
+
+        def store(h):
+            o_b = results[h][:].rearrange("p (h b x) -> p h b x", h=2, b=2)
+            for b in range(2):
+                nc.sync.dma_start(out=unit_out(h, b), in_=o_b[:, :, b, :])
+
+        terms = {}
+
+        def products(h, b):
+            if h not in results:
+                results[h] = out_pool.tile([P, 1024], F32, name="o_t")
+            if h >= FIRST_V_UNIT:
+                o_v = results[h][:].rearrange("p (h t d) -> p t h d", h=2, t=4)
+                nc.scalar.copy(
+                    out=o_v[:, 2 * b : 2 * b + 2],
+                    in_=sums[(h, b)][:].rearrange("p (e h d) -> p e h d", e=2, h=2),
+                )
+                return
+            if h not in terms:
+                terms[h] = tt_pool.tile([P, 2048], F32, name="t_t")
+            tt5 = terms[h][:].rearrange("p (b q s j) -> p b q s j", b=2, q=4, s=4)
+            acc4 = sums[(h, b)][:].rearrange("p (q f j) -> p q f j", q=4, f=2)
+            nc.vector.tensor_tensor(
+                out=tt5[:, b, :, 0:4:3, :],
+                in0=acc4[:, :, 0:1, :].to_broadcast([P, 4, 2, 64]),
+                in1=tab_r[:, 0, b],
+                op=MULT,
+            )
+            nc.vector.tensor_tensor(
+                out=tt5[:, b, :, 1:3, :],
+                in0=acc4[:, :, 1:2, :].to_broadcast([P, 4, 2, 64]),
+                in1=tab_r[:, 1, b],
+                op=MULT,
+            )
+
+        def combine(h):
+            if h >= FIRST_V_UNIT:
+                return
+            o_v = results[h][:].rearrange("p (h t d) -> p t h d", h=2, t=4)
+            tt_u = terms[h][:].rearrange("p (t h s j) -> p t h s j", t=4, h=2, s=4)
+            eng = nc.vector if h in VECTOR_ADDS else nc.gpsimd
+            eng.tensor_tensor(
+                out=o_v,
+                in0=tt_u[:, :, :, 0:2, :].rearrange("p t h f j -> p t h (f j)"),
+                in1=tt_u[:, :, :, 2:4, :].rearrange("p t h f j -> p t h (f j)"),
+                op=ADD,
+            )
+
+        def finish(h):
+            products(h, 0)
+            products(h, 1)
+            combine(h)
+
+        ALL = (0, 1, 2, 3)
+
+        for h in (0, 2, 1):
+            head_half(h, 0)
+            head_half(h, 1)
+        multiply(2, (0,))
+        transposes(3, (0, 1))
+        evacuate(3, (0, 1), (1,))
+        build_tables()
+        quantise(3, ((0, 512),))
+        multiply(2, (1,))
+        transposes(3, (2, 3))
+        evacuate(3, (2, 3), ())
+        products(2, 0)
+        quantise(3, ((512, 1024),))
+        transposes(4, ALL)
+        evacuate(4, ALL, ())
+        products(2, 1)
+        combine(2)
+        store(2)
+        multiply(3, (0,))
+        transposes(5, ALL)
+        evacuate(5, ALL, ())
+        quantise(4, WHOLE)
+        multiply(3, (1,))
+        transposes(6, (0, 1))
+        evacuate(6, (0, 1), ())
+        finish(3)
+        store(3)
+        quantise(5, WHOLE)
+        multiply(4, (0,))
+        transposes(6, (2, 3))
+        evacuate(6, (2, 3), ())
+        multiply(4, (1,))
+        for m in range(5, 14):
+            if m + 2 <= 13:
+                transposes(m + 2, (0, 1))
+                evacuate(m + 2, (0, 1), ())
+            if m == 12:
+                quantise(13, WHOLE)
+            finish(m - 1)
+            if m - 1 != 11:
+                store(m - 1)
+            if m - 1 == 12:
+                store(11)
+            if m + 1 <= 12:
+                quantise(m + 1, WHOLE)
+            multiply(m, (0,))
+            if m + 2 <= 13:
+                transposes(m + 2, (2, 3))
+                evacuate(m + 2, (2, 3), ())
+            multiply(m, (1,))
+        finish(13)
+        store(13)

@@ -16,7 +16,8 @@ ADD = mybir.AluOpType.add
 P = 128
 LOAD_ORDER = (0, 2, 1, 3, 4, 5, 6, 7, 8, 9, 10, 11, 12, 13)
 HALVED = (0, 1, 2, 3)
-VECTOR_ADDS = (2, 11)
+VECTOR_ADDS = (2,)
+PERMUTED = (5, 6, 7, 8, 9, 10, 11, 12, 13)
 FIRST_V_UNIT = 12
 
 
@@ -28,10 +29,11 @@ def tile_mistralattention_kernel(
         src_pool = ctx.enter_context(tc.tile_pool(name="src", bufs=1))
         const_pool = ctx.enter_context(tc.tile_pool(name="const", bufs=1))
         grp_pool = ctx.enter_context(tc.tile_pool(name="grp", bufs=3))
+        perm_pool = ctx.enter_context(tc.tile_pool(name="perm", bufs=3))
         xq_pool = ctx.enter_context(tc.tile_pool(name="xq", bufs=1))
         wq_pool = ctx.enter_context(tc.tile_pool(name="wq", bufs=3))
-        tt_pool = ctx.enter_context(tc.tile_pool(name="tt", bufs=3))
-        out_pool = ctx.enter_context(tc.tile_pool(name="outp", bufs=7))
+        tt_pool = ctx.enter_context(tc.tile_pool(name="tt", bufs=4))
+        out_pool = ctx.enter_context(tc.tile_pool(name="outp", bufs=6))
         tp_pool = ctx.enter_context(tc.psum_pool(name="tp", bufs=4))
         acc_pool = ctx.enter_context(tc.psum_pool(name="acc", bufs=4))
         ctx.enter_context(tc.manual_schedule())
@@ -88,7 +90,22 @@ def tile_mistralattention_kernel(
                     in_=sin.rearrange("b (p e) d -> p b (e d)", e=2),
                 )
 
+        permuted = {}
+
+        def permute(h, lo, hi, eng):
+            if h not in permuted:
+                permuted[h] = perm_pool.tile([P, 2048], F32, name="perm_t")
+            s_v = src[(h, 0)][:].bitcast(F32).rearrange("p (r g q u) -> p r g u q", r=2, g=4, u=2)
+            d_v = permuted[h][:].rearrange("p (r g u q) -> p r g u q", r=2, g=4, u=2)
+            if eng == "scalar":
+                nc.scalar.copy(out=d_v[:, :, lo:hi], in_=s_v[:, :, lo:hi])
+            else:
+                nc.vector.tensor_copy(out=d_v[:, :, lo:hi], in_=s_v[:, :, lo:hi])
+
         def src_words(h, g, u, r):
+            if h in PERMUTED:
+                col = 1024 * r + 256 * g + 128 * u
+                return permuted[h][:, col : col + 128]
             if h in HALVED:
                 s_f = src[(h, g // 2)][:].bitcast(F32)
                 col = 512 * r + 256 * (g % 2)
@@ -190,10 +207,9 @@ def tile_mistralattention_kernel(
 
         results = {}
 
-        def store(h):
+        def store(h, b):
             o_b = results[h][:].rearrange("p (h b x) -> p h b x", h=2, b=2)
-            for b in range(2):
-                nc.sync.dma_start(out=unit_out(h, b), in_=o_b[:, :, b, :])
+            nc.sync.dma_start(out=unit_out(h, b), in_=o_b[:, :, b, :])
 
         terms = {}
 
@@ -207,40 +223,39 @@ def tile_mistralattention_kernel(
                     in_=sums[(h, b)][:].rearrange("p (e h d) -> p e h d", e=2, h=2),
                 )
                 return
-            if h not in terms:
-                terms[h] = tt_pool.tile([P, 2048], F32, name="t_t")
-            tt5 = terms[h][:].rearrange("p (b q s j) -> p b q s j", b=2, q=4, s=4)
+            terms[(h, b)] = tt_pool.tile([P, 1024], F32, name="t_t")
+            tt5 = terms[(h, b)][:].rearrange("p (q s j) -> p q s j", q=4, s=4)
             acc4 = sums[(h, b)][:].rearrange("p (q f j) -> p q f j", q=4, f=2)
             nc.vector.tensor_tensor(
-                out=tt5[:, b, :, 0:4:3, :],
+                out=tt5[:, :, 0:4:3, :],
                 in0=acc4[:, :, 0:1, :].to_broadcast([P, 4, 2, 64]),
                 in1=tab_r[:, 0, b],
                 op=MULT,
             )
             nc.vector.tensor_tensor(
-                out=tt5[:, b, :, 1:3, :],
+                out=tt5[:, :, 1:3, :],
                 in0=acc4[:, :, 1:2, :].to_broadcast([P, 4, 2, 64]),
                 in1=tab_r[:, 1, b],
                 op=MULT,
             )
 
-        def combine(h):
+        def combine(h, b):
             if h >= FIRST_V_UNIT:
                 return
             o_v = results[h][:].rearrange("p (h t d) -> p t h d", h=2, t=4)
-            tt_u = terms[h][:].rearrange("p (t h s j) -> p t h s j", t=4, h=2, s=4)
+            tt_u = terms[(h, b)][:].rearrange("p (t h s j) -> p t h s j", t=2, h=2, s=4)
             eng = nc.vector if h in VECTOR_ADDS else nc.gpsimd
             eng.tensor_tensor(
-                out=o_v,
+                out=o_v[:, 2 * b : 2 * b + 2],
                 in0=tt_u[:, :, :, 0:2, :].rearrange("p t h f j -> p t h (f j)"),
                 in1=tt_u[:, :, :, 2:4, :].rearrange("p t h f j -> p t h (f j)"),
                 op=ADD,
             )
 
-        def finish(h):
-            products(h, 0)
-            products(h, 1)
-            combine(h)
+        def finish(h, b):
+            products(h, b)
+            combine(h, b)
+            store(h, b)
 
         ALL = (0, 1, 2, 3)
 
@@ -260,17 +275,26 @@ def tile_mistralattention_kernel(
         transposes(4, ALL)
         evacuate(4, ALL, ())
         products(2, 1)
-        combine(2)
-        store(2)
+        combine(2, 0)
+        store(2, 0)
+        combine(2, 1)
+        store(2, 1)
+        permute(5, 0, 2, "scalar")
+        permute(5, 2, 4, "vector")
         multiply(3, (0,))
         transposes(5, ALL)
-        evacuate(5, ALL, ())
+        evacuate(5, (0, 1), ())
+        permute(6, 0, 2, "scalar")
+        evacuate(5, (2, 3), ())
+        permute(6, 2, 4, "vector")
         quantise(4, WHOLE)
         multiply(3, (1,))
         transposes(6, (0, 1))
         evacuate(6, (0, 1), ())
-        finish(3)
-        store(3)
+        permute(7, 0, 2, "scalar")
+        finish(3, 0)
+        permute(7, 2, 4, "vector")
+        finish(3, 1)
         quantise(5, WHOLE)
         multiply(4, (0,))
         transposes(6, (2, 3))
@@ -280,13 +304,14 @@ def tile_mistralattention_kernel(
             if m + 2 <= 13:
                 transposes(m + 2, (0, 1))
                 evacuate(m + 2, (0, 1), ())
+            if m + 3 <= 13:
+                permute(m + 3, 0, 2, "scalar")
             if m == 12:
                 quantise(13, WHOLE)
-            finish(m - 1)
-            if m - 1 != 11:
-                store(m - 1)
-            if m - 1 == 12:
-                store(11)
+            finish(m - 1, 0)
+            if m + 3 <= 13:
+                permute(m + 3, 2, 4, "vector")
+            finish(m - 1, 1)
             if m + 1 <= 12:
                 quantise(m + 1, WHOLE)
             multiply(m, (0,))
@@ -294,5 +319,5 @@ def tile_mistralattention_kernel(
                 transposes(m + 2, (2, 3))
                 evacuate(m + 2, (2, 3), ())
             multiply(m, (1,))
-        finish(13)
-        store(13)
+        finish(13, 0)
+        finish(13, 1)

@@ -17,7 +17,7 @@ P = 128
 LOAD_ORDER = (0, 2, 1, 3, 4, 5, 6, 7, 8, 9, 10, 11, 12, 13)
 HALVED = (0, 1, 2, 3)
 VECTOR_ADDS = (2,)
-PERMUTED = (5, 6, 7, 8, 9, 10, 11, 12, 13)
+PERMUTED = (6, 7, 8, 9, 10, 11, 12, 13)
 FIRST_V_UNIT = 12
 
 
@@ -92,19 +92,15 @@ def tile_mistralattention_kernel(
 
         permuted = {}
 
-        def permute(h, lo, hi, eng):
-            if h not in permuted:
-                permuted[h] = perm_pool.tile([P, 2048], F32, name="perm_t")
+        def permute(h):
+            permuted[h] = perm_pool.tile([P, 1024], F32, name="perm_t")
             s_v = src[(h, 0)][:].bitcast(F32).rearrange("p (r g q u) -> p r g u q", r=2, g=4, u=2)
-            d_v = permuted[h][:].rearrange("p (r g u q) -> p r g u q", r=2, g=4, u=2)
-            if eng == "scalar":
-                nc.scalar.copy(out=d_v[:, :, lo:hi], in_=s_v[:, :, lo:hi])
-            else:
-                nc.vector.tensor_copy(out=d_v[:, :, lo:hi], in_=s_v[:, :, lo:hi])
+            d_v = permuted[h][:].rearrange("p (r g u q) -> p r g u q", r=2, g=2, u=2)
+            nc.scalar.copy(out=d_v, in_=s_v[:, :, 0:2])
 
         def src_words(h, g, u, r):
-            if h in PERMUTED:
-                col = 1024 * r + 256 * g + 128 * u
+            if h in PERMUTED and g < 2:
+                col = 512 * r + 256 * g + 128 * u
                 return permuted[h][:, col : col + 128]
             if h in HALVED:
                 s_f = src[(h, g // 2)][:].bitcast(F32)
@@ -279,21 +275,17 @@ def tile_mistralattention_kernel(
         store(2, 0)
         combine(2, 1)
         store(2, 1)
-        permute(5, 0, 2, "scalar")
-        permute(5, 2, 4, "vector")
         multiply(3, (0,))
         transposes(5, ALL)
         evacuate(5, (0, 1), ())
-        permute(6, 0, 2, "scalar")
+        permute(6)
         evacuate(5, (2, 3), ())
-        permute(6, 2, 4, "vector")
         quantise(4, WHOLE)
         multiply(3, (1,))
         transposes(6, (0, 1))
         evacuate(6, (0, 1), ())
-        permute(7, 0, 2, "scalar")
+        permute(7)
         finish(3, 0)
-        permute(7, 2, 4, "vector")
         finish(3, 1)
         quantise(5, WHOLE)
         multiply(4, (0,))
@@ -305,12 +297,10 @@ def tile_mistralattention_kernel(
                 transposes(m + 2, (0, 1))
                 evacuate(m + 2, (0, 1), ())
             if m + 3 <= 13:
-                permute(m + 3, 0, 2, "scalar")
+                permute(m + 3)
             if m == 12:
                 quantise(13, WHOLE)
             finish(m - 1, 0)
-            if m + 3 <= 13:
-                permute(m + 3, 2, 4, "vector")
             finish(m - 1, 1)
             if m + 1 <= 12:
                 quantise(m + 1, WHOLE)

@@ -16,7 +16,7 @@ ADD = mybir.AluOpType.add
 P = 128
 LOAD_ORDER = (0, 2, 1, 3, 4, 5, 6, 7, 8, 9, 10, 11, 12, 13)
 HALVED = (0, 1, 2, 3)
-VECTOR_ADDS = (2,)
+VECTOR_ADDS = (2, 11)
 PERMUTED = (6, 7, 8, 9, 10, 11, 12, 13)
 FIRST_V_UNIT = 12
 
@@ -32,7 +32,7 @@ def tile_mistralattention_kernel(
         perm_pool = ctx.enter_context(tc.tile_pool(name="perm", bufs=3))
         xq_pool = ctx.enter_context(tc.tile_pool(name="xq", bufs=1))
         wq_pool = ctx.enter_context(tc.tile_pool(name="wq", bufs=3))
-        tt_pool = ctx.enter_context(tc.tile_pool(name="tt", bufs=4))
+        tt_pool = ctx.enter_context(tc.tile_pool(name="tt", bufs=2))
         out_pool = ctx.enter_context(tc.tile_pool(name="outp", bufs=6))
         tp_pool = ctx.enter_context(tc.psum_pool(name="tp", bufs=4))
         acc_pool = ctx.enter_context(tc.psum_pool(name="acc", bufs=4))
@@ -219,8 +219,9 @@ def tile_mistralattention_kernel(
                     in_=sums[(h, b)][:].rearrange("p (e h d) -> p e h d", e=2, h=2),
                 )
                 return
-            terms[(h, b)] = tt_pool.tile([P, 1024], F32, name="t_t")
-            tt5 = terms[(h, b)][:].rearrange("p (q s j) -> p q s j", q=4, s=4)
+            if h not in terms:
+                terms[h] = tt_pool.tile([P, 2048], F32, name="t_t")
+            tt5 = terms[h][:].rearrange("p (b q s j) -> p b q s j", b=2, q=4, s=4)[:, b]
             acc4 = sums[(h, b)][:].rearrange("p (q f j) -> p q f j", q=4, f=2)
             nc.vector.tensor_tensor(
                 out=tt5[:, :, 0:4:3, :],
@@ -235,23 +236,25 @@ def tile_mistralattention_kernel(
                 op=MULT,
             )
 
-        def combine(h, b):
+        def combine(h):
             if h >= FIRST_V_UNIT:
                 return
             o_v = results[h][:].rearrange("p (h t d) -> p t h d", h=2, t=4)
-            tt_u = terms[(h, b)][:].rearrange("p (t h s j) -> p t h s j", t=2, h=2, s=4)
+            tt_u = terms[h][:].rearrange("p (t h s j) -> p t h s j", t=4, h=2, s=4)
             eng = nc.vector if h in VECTOR_ADDS else nc.gpsimd
             eng.tensor_tensor(
-                out=o_v[:, 2 * b : 2 * b + 2],
+                out=o_v,
                 in0=tt_u[:, :, :, 0:2, :].rearrange("p t h f j -> p t h (f j)"),
                 in1=tt_u[:, :, :, 2:4, :].rearrange("p t h f j -> p t h (f j)"),
                 op=ADD,
             )
 
-        def finish(h, b):
-            products(h, b)
-            combine(h, b)
-            store(h, b)
+        def finish(h):
+            products(h, 0)
+            products(h, 1)
+            combine(h)
+            store(h, 0)
+            store(h, 1)
 
         ALL = (0, 1, 2, 3)
 
@@ -271,9 +274,8 @@ def tile_mistralattention_kernel(
         transposes(4, ALL)
         evacuate(4, ALL, ())
         products(2, 1)
-        combine(2, 0)
+        combine(2)
         store(2, 0)
-        combine(2, 1)
         store(2, 1)
         multiply(3, (0,))
         transposes(5, ALL)
@@ -285,8 +287,7 @@ def tile_mistralattention_kernel(
         transposes(6, (0, 1))
         evacuate(6, (0, 1), ())
         permute(7)
-        finish(3, 0)
-        finish(3, 1)
+        finish(3)
         quantise(5, WHOLE)
         multiply(4, (0,))
         transposes(6, (2, 3))
@@ -300,8 +301,7 @@ def tile_mistralattention_kernel(
                 permute(m + 3)
             if m == 12:
                 quantise(13, WHOLE)
-            finish(m - 1, 0)
-            finish(m - 1, 1)
+            finish(m - 1)
             if m + 1 <= 12:
                 quantise(m + 1, WHOLE)
             multiply(m, (0,))
@@ -309,5 +309,4 @@ def tile_mistralattention_kernel(
                 transposes(m + 2, (2, 3))
                 evacuate(m + 2, (2, 3), ())
             multiply(m, (1,))
-        finish(13, 0)
-        finish(13, 1)
+        finish(13)

@@ -205,7 +205,8 @@ def tile_mistralattention_kernel(
 
         def store(h, b):
             o_b = results[h][:].rearrange("p (h b x) -> p h b x", h=2, b=2)
-            nc.sync.dma_start(out=unit_out(h, b), in_=o_b[:, :, b, :])
+            queue = nc.scalar if h >= FIRST_V_UNIT else nc.sync
+            queue.dma_start(out=unit_out(h, b), in_=o_b[:, :, b, :])
 
         terms = {}
 
@@ -299,9 +300,16 @@ def tile_mistralattention_kernel(
                 evacuate(m + 2, (0, 1), ())
             if m + 3 <= 13:
                 permute(m + 3)
+            products(m - 1, 0)
+            if m - 1 >= FIRST_V_UNIT:
+                store(m - 1, 0)
+            products(m - 1, 1)
             if m == 12:
                 quantise(13, WHOLE)
-            finish(m - 1)
+            combine(m - 1)
+            if m - 1 < FIRST_V_UNIT:
+                store(m - 1, 0)
+            store(m - 1, 1)
             if m + 1 <= 12:
                 quantise(m + 1, WHOLE)
             multiply(m, (0,))
@@ -309,4 +317,7 @@ def tile_mistralattention_kernel(
                 transposes(m + 2, (2, 3))
                 evacuate(m + 2, (2, 3), ())
             multiply(m, (1,))
-        finish(13)
+        products(13, 0)
+        store(13, 0)
+        products(13, 1)
+        store(13, 1)

@@ -14,10 +14,11 @@ MULT = mybir.AluOpType.mult
 ADD = mybir.AluOpType.add
 
 P = 128
+UNITS = 14
+LAST = 13
 LOAD_ORDER = (0, 2, 1, 3, 4, 5, 6, 7, 8, 9, 10, 11, 12, 13)
-HALVED = (0, 1, 2, 3)
-VECTOR_ADDS = (2, 11)
-PERMUTED = (6, 7, 8, 9, 10, 11, 12, 13)
+SPLIT = (0, 1, 2, 3)
+FIRST_PERMUTED = 5
 FIRST_V_UNIT = 12
 
 
@@ -28,12 +29,12 @@ def tile_mistralattention_kernel(
     with ExitStack() as ctx:
         src_pool = ctx.enter_context(tc.tile_pool(name="src", bufs=1))
         const_pool = ctx.enter_context(tc.tile_pool(name="const", bufs=1))
+        perm_pool = ctx.enter_context(tc.tile_pool(name="perm", bufs=6))
         grp_pool = ctx.enter_context(tc.tile_pool(name="grp", bufs=3))
-        perm_pool = ctx.enter_context(tc.tile_pool(name="perm", bufs=3))
         xq_pool = ctx.enter_context(tc.tile_pool(name="xq", bufs=1))
         wq_pool = ctx.enter_context(tc.tile_pool(name="wq", bufs=3))
-        tt_pool = ctx.enter_context(tc.tile_pool(name="tt", bufs=2))
-        out_pool = ctx.enter_context(tc.tile_pool(name="outp", bufs=6))
+        term_pool = ctx.enter_context(tc.tile_pool(name="term", bufs=2))
+        out_pool = ctx.enter_context(tc.tile_pool(name="outp", bufs=5))
         tp_pool = ctx.enter_context(tc.psum_pool(name="tp", bufs=4))
         acc_pool = ctx.enter_context(tc.psum_pool(name="acc", bufs=4))
         ctx.enter_context(tc.manual_schedule())
@@ -53,12 +54,10 @@ def tile_mistralattention_kernel(
         def unit_out(h, b):
             w = h - 2
             if w < 8:
-                dst = out_0[b, 2 * w : 2 * w + 2]
-            elif w < 10:
-                dst = out_1[b, 2 * (w - 8) : 2 * (w - 8) + 2]
-            else:
-                dst = out_2[b, 2 * (w - 10) : 2 * (w - 10) + 2]
-            return dst.rearrange("h (p e) d -> p h (e d)", e=2)
+                return out_0[b, 2 * w : 2 * w + 2]
+            if w < 10:
+                return out_1[b, 2 * (w - 8) : 2 * (w - 8) + 2]
+            return out_2[b, 2 * (w - 10) : 2 * (w - 10) + 2]
 
         ident = const_pool.tile([P, P], F32, name="ident")
         make_identity(nc, ident[:])
@@ -68,101 +67,104 @@ def tile_mistralattention_kernel(
         src = {}
         for h in LOAD_ORDER:
             rows = unit_rows(h)
-            if h in HALVED:
-                for i in range(2):
-                    s_t = src_pool.tile([P, 2048], BF16, name="src%d_%d" % (h, i))
-                    src[(h, i)] = s_t
-                    nc.sync.dma_start(
-                        out=s_t[:].rearrange("p (r k) -> p r k", r=2),
-                        in_=rows[:, :, 1024 * i : 1024 * i + 1024],
-                    )
+            if h in SPLIT:
+                for r in range(2):
+                    s_t = src_pool.tile([P, 2048], BF16, name="src%d_%d" % (h, r))
+                    src[(h, r)] = s_t
+                    nc.sync.dma_start(out=s_t[:], in_=rows[:, r, :])
             else:
                 s_t = src_pool.tile([P, 4096], BF16, name="src%d" % h)
-                src[(h, 0)] = s_t
+                src[h] = s_t
                 nc.sync.dma_start(out=s_t[:].rearrange("p (r k) -> p r k", r=2), in_=rows)
             if h == 3:
-                nc.sync.dma_start(
-                    out=cos_sb[:].rearrange("p (b x) -> p b x", b=2),
-                    in_=cos.rearrange("b (p e) d -> p b (e d)", e=2),
-                )
-                nc.sync.dma_start(
-                    out=sin_sb[:].rearrange("p (b x) -> p b x", b=2),
-                    in_=sin.rearrange("b (p e) d -> p b (e d)", e=2),
-                )
-
-        permuted = {}
-
-        def permute(h):
-            permuted[h] = perm_pool.tile([P, 1024], F32, name="perm_t")
-            s_v = src[(h, 0)][:].bitcast(F32).rearrange("p (r g q u) -> p r g u q", r=2, g=4, u=2)
-            d_v = permuted[h][:].rearrange("p (r g u q) -> p r g u q", r=2, g=2, u=2)
-            nc.scalar.copy(out=d_v, in_=s_v[:, :, 0:2])
-
-        def src_words(h, g, u, r):
-            if h in PERMUTED and g < 2:
-                col = 512 * r + 256 * g + 128 * u
-                return permuted[h][:, col : col + 128]
-            if h in HALVED:
-                s_f = src[(h, g // 2)][:].bitcast(F32)
-                col = 512 * r + 256 * (g % 2)
-            else:
-                s_f = src[(h, 0)][:].bitcast(F32)
-                col = 1024 * r + 256 * g
-            return s_f[:, col + u : col + 256 : 2]
+                for table, source in ((cos_sb, cos), (sin_sb, sin)):
+                    nc.sync.dma_start(
+                        out=table[:].rearrange("p (b x) -> p b x", b=2),
+                        in_=source.rearrange("b (p e) d -> p b (e d)", e=2),
+                    )
 
         tab = const_pool.tile([P, 2048], F32, name="tab")
-        tab_w = tab[:].rearrange("p (a t h c j) -> p a t h c j", a=2, t=4, h=2, c=2)
-        tab_r = tab[:].rearrange("p (a b q c j) -> p a b q c j", a=2, b=2, q=4, c=2)
+        tab_w = tab[:].rearrange("p (f t h c j) -> p f t h c j", f=2, t=4, h=2, c=2)
+        tab_r = tab[:].rearrange("p (f b q c j) -> p f b q c j", f=2, b=2, q=4, c=2)
         cos_v = cos_sb[:].rearrange("p (t f j) -> p t f j", t=4, f=2)
         sin_v = sin_sb[:].rearrange("p (t f j) -> p t f j", t=4, f=2)
 
         def build_tables():
-            for eng, a, c, view, f, sign in (
+            for eng, f, c, view, half, sign in (
                 (nc.vector, 0, 0, cos_v, 0, 1.0),
                 (nc.gpsimd, 0, 1, sin_v, 1, 1.0),
-                (nc.vector, 1, 0, cos_v, 1, 1.0),
-                (nc.gpsimd, 1, 1, sin_v, 0, -1.0),
+                (nc.vector, 1, 1, cos_v, 1, 1.0),
+                (nc.gpsimd, 1, 0, sin_v, 0, -1.0),
             ):
                 eng.tensor_scalar(
-                    out=tab_w[:, a, :, :, c, :],
-                    in0=view[:, :, f, :].unsqueeze(2).to_broadcast([P, 4, 2, 64]),
+                    out=tab_w[:, f, :, :, c, :],
+                    in0=view[:, :, half, :].unsqueeze(2).to_broadcast([P, 4, 2, 64]),
                     scalar1=sign,
                     scalar2=0.0,
                     op0=MULT,
                     op1=ADD,
                 )
 
+        permuted = {}
         grouped = {}
         codes = {}
         planes = {}
-        banks = {}
         sums = {}
+        results = {}
+        terms = {}
 
-        def transposes(h, gs):
+        def permute(h, i):
+            if i == 1 and h % 2 == 0:
+                return
+            t = perm_pool.tile([P, 1024], F32, name="perm_t")
+            permuted[(h, i)] = t
+            words = src[h][:].bitcast(F32).rearrange("p (r g q u) -> p r g u q", r=2, g=4, u=2)
+            source = words[:, :, 2 * i : 2 * i + 2]
+            target = t[:].rearrange("p (r g u q) -> p r g u q", r=2, g=2, u=2)
+            if i == 0:
+                nc.scalar.copy(out=target, in_=source)
+            else:
+                nc.vector.tensor_copy(out=target, in_=source)
+
+        def words(h, g, u, r):
+            if (h, g // 2) in permuted:
+                col = 512 * r + 256 * (g % 2) + 128 * u
+                return permuted[(h, g // 2)][:, col : col + 128]
+            if h in SPLIT:
+                col = 256 * g
+                return src[(h, r)][:].bitcast(F32)[:, col + u : col + 256 : 2]
+            col = 1024 * r + 256 * g
+            return src[h][:].bitcast(F32)[:, col + u : col + 256 : 2]
+
+        def transposes(h, i):
             if h not in grouped:
                 grouped[h] = grp_pool.tile([P, 4096], BF16, name="grp", align_bytes=64)
-            for g in gs:
-                pt = tp_pool.tile([P, 512], F32, name="pt")
-                banks[(h, g)] = pt
-                for u in range(2):
-                    for r in range(2):
-                        nc.tensor.transpose(
-                            pt[:, 256 * u + 128 * r : 256 * u + 128 * r + 128],
-                            src_words(h, g, u, r),
-                            ident[:],
-                        )
-
-        def evacuate(h, gs, vector_gs):
             g_f = grouped[h][:].bitcast(F32)
-            for g in gs:
-                dst = g_f[:, 512 * g : 512 * g + 512].rearrange("p (o u) -> p o u", u=2)
-                view = banks[(h, g)][:].rearrange("p (u o) -> p o u", u=2)
-                if g in vector_gs:
-                    nc.vector.tensor_copy(out=dst, in_=view)
+            for q in range(2):
+                bank = tp_pool.tile([P, 512], F32, name="bank")
+                for y in range(2):
+                    for u in range(2):
+                        if h in SPLIT:
+                            place, source = 256 * y + 128 * u, words(h, 2 * q + y, u, i)
+                        else:
+                            place, source = 256 * u + 128 * y, words(h, 2 * i + q, u, y)
+                        nc.tensor.transpose(bank[:, place : place + 128], source, ident[:])
+                if h < 2:
+                    col = 1024 * i + 512 * q
+                    dst = g_f[:, col : col + 512].rearrange("p (y o u) -> p y o u", y=2, u=2)
+                elif h in SPLIT:
+                    dst = g_f.rearrange("p (g r o u) -> p r g o u", g=4, r=2, u=2)
+                    dst = dst[:, i, 2 * q : 2 * q + 2]
                 else:
-                    nc.scalar.copy(out=dst, in_=view)
+                    col = 512 * (2 * i + q)
+                    dst = g_f[:, col : col + 512].rearrange("p (o u) -> p o u", u=2)
+                if h in SPLIT:
+                    view = bank[:].rearrange("p (y u o) -> p y o u", y=2, u=2)
+                else:
+                    view = bank[:].rearrange("p (u o) -> p o u", u=2)
+                nc.scalar.copy(out=dst, in_=view)
 
-        def quantise(h, parts):
+        def quantise(h, parts=((0, 1024),)):
             if h not in codes:
                 pool = xq_pool if h < 2 else wq_pool
                 tag = "x%d" % h if h < 2 else "w"
@@ -175,149 +177,146 @@ def tile_mistralattention_kernel(
                     in_=grouped[h][:, 4 * lo : 4 * hi],
                 )
 
-        WHOLE = ((0, 1024),)
+        def quantise_rows(h, r):
+            if h < 2:
+                quantise(h, ((512 * r, 512 * r + 512),))
+            else:
+                quantise(h, tuple((256 * g + 128 * r, 256 * g + 128 * r + 128) for g in range(4)))
 
-        def head_half(h, i):
-            gs = (2 * i, 2 * i + 1)
-            transposes(h, gs)
-            evacuate(h, gs, (2 * i + 1,))
-            quantise(h, ((512 * i, 512 * i + 512),))
+        def multiply(h, b, es=(0, 1)):
+            for e in es:
+                if e == 0 or (h, b) == (LAST, 1):
+                    sums[(h, b, e)] = acc_pool.tile([P, 512], F32, name="acc")
+                else:
+                    sums[(h, b, e)] = sums[(h, b, 0)]
+                acc = sums[(h, b, e)]
+                for g in range(4):
+                    xs = slice(512 * e + 128 * g, 512 * e + 128 * g + 128)
+                    ws = slice(256 * g, 256 * g + 256)
+                    nc.tensor.matmul_mx(
+                        out=acc[:, 256 * e : 256 * e + 256],
+                        lhsT=codes[b][:, xs].bitcast(FP8X4),
+                        lhsT_scale=planes[b][:, xs],
+                        rhs=codes[h][:, ws].bitcast(FP8X4),
+                        rhs_scale=planes[h][:, ws],
+                        start=(g == 0),
+                        stop=(g == 3),
+                    )
 
-        def multiply(h, bs):
-            for b in bs:
-                acc = acc_pool.tile([P, 512], F32, name="acc")
-                sums[(h, b)] = acc
-                for e in range(2):
-                    for g in range(4):
-                        xs = slice(256 * g + 128 * e, 256 * g + 128 * e + 128)
-                        ws = slice(256 * g, 256 * g + 256)
-                        nc.tensor.matmul_mx(
-                            out=acc[:, 256 * e : 256 * e + 256],
-                            lhsT=codes[b][:, xs].bitcast(FP8X4),
-                            lhsT_scale=planes[b][:, xs],
-                            rhs=codes[h][:, ws].bitcast(FP8X4),
-                            rhs_scale=planes[h][:, ws],
-                            start=(g == 0),
-                            stop=(g == 3),
-                        )
+        def result_tile(h):
+            if h not in results:
+                results[h] = out_pool.tile([P, 1024], F32, name="o_t")
+            return results[h][:].rearrange("p (h t d) -> p t h d", h=2, t=4)
 
-        results = {}
+        def products(h, b):
+            if h not in terms:
+                terms[h] = term_pool.tile([P, 2048], F32, name="t_t")
+            t_v = terms[h][:].rearrange("p (f b q c j) -> p f b q c j", f=2, b=2, q=4, c=2)
+            acc_v = sums[(h, b, 0)][:].rearrange("p (q f j) -> p q f j", q=4, f=2)
+            for f in range(2):
+                nc.vector.tensor_tensor(
+                    out=t_v[:, f, b],
+                    in0=acc_v[:, :, f : f + 1, :].to_broadcast([P, 4, 2, 64]),
+                    in1=tab_r[:, f, b],
+                    op=MULT,
+                )
+
+        def combine(h, ts, eng):
+            t_v = terms[h][:].rearrange("p (f t h d) -> p f t h d", f=2, t=4, h=2)
+            eng.tensor_tensor(
+                out=result_tile(h)[:, ts], in0=t_v[:, 0, ts], in1=t_v[:, 1, ts], op=ADD
+            )
 
         def store(h, b):
             o_b = results[h][:].rearrange("p (h b x) -> p h b x", h=2, b=2)
             queue = nc.scalar if h >= FIRST_V_UNIT else nc.sync
-            queue.dma_start(out=unit_out(h, b), in_=o_b[:, :, b, :])
-
-        terms = {}
-
-        def products(h, b):
-            if h not in results:
-                results[h] = out_pool.tile([P, 1024], F32, name="o_t")
-            if h >= FIRST_V_UNIT:
-                o_v = results[h][:].rearrange("p (h t d) -> p t h d", h=2, t=4)
-                nc.scalar.copy(
-                    out=o_v[:, 2 * b : 2 * b + 2],
-                    in_=sums[(h, b)][:].rearrange("p (e h d) -> p e h d", e=2, h=2),
-                )
-                return
-            if h not in terms:
-                terms[h] = tt_pool.tile([P, 2048], F32, name="t_t")
-            tt5 = terms[h][:].rearrange("p (b q s j) -> p b q s j", b=2, q=4, s=4)[:, b]
-            acc4 = sums[(h, b)][:].rearrange("p (q f j) -> p q f j", q=4, f=2)
-            nc.vector.tensor_tensor(
-                out=tt5[:, :, 0:4:3, :],
-                in0=acc4[:, :, 0:1, :].to_broadcast([P, 4, 2, 64]),
-                in1=tab_r[:, 0, b],
-                op=MULT,
-            )
-            nc.vector.tensor_tensor(
-                out=tt5[:, :, 1:3, :],
-                in0=acc4[:, :, 1:2, :].to_broadcast([P, 4, 2, 64]),
-                in1=tab_r[:, 1, b],
-                op=MULT,
+            queue.dma_start(
+                out=unit_out(h, b).rearrange("h (p e) d -> p h (e d)", e=2), in_=o_b[:, :, b, :]
             )
 
-        def combine(h):
-            if h >= FIRST_V_UNIT:
-                return
-            o_v = results[h][:].rearrange("p (h t d) -> p t h d", h=2, t=4)
-            tt_u = terms[h][:].rearrange("p (t h s j) -> p t h s j", t=4, h=2, s=4)
-            eng = nc.vector if h in VECTOR_ADDS else nc.gpsimd
-            eng.tensor_tensor(
-                out=o_v,
-                in0=tt_u[:, :, :, 0:2, :].rearrange("p t h f j -> p t h (f j)"),
-                in1=tt_u[:, :, :, 2:4, :].rearrange("p t h f j -> p t h (f j)"),
-                op=ADD,
-            )
+        WHOLE = slice(0, 4)
+        HALF = (slice(0, 2), slice(2, 4))
 
         def finish(h):
             products(h, 0)
             products(h, 1)
-            combine(h)
+            combine(h, WHOLE, nc.gpsimd)
             store(h, 0)
             store(h, 1)
 
-        ALL = (0, 1, 2, 3)
+        def finish_halves(h, q):
+            products(h, 0)
+            combine(h, HALF[0], nc.gpsimd)
+            store(h, 0)
+            products(h, 1)
+            quantise(q)
+            combine(h, HALF[1], nc.vector)
+            store(h, 1)
+
+        def finish_v(h, b):
+            o_v = result_tile(h)
+            acc_v = sums[(h, b, 0)][:].rearrange("p (e h d) -> p e h d", e=2, h=2)
+            nc.scalar.copy(out=o_v[:, HALF[b]], in_=acc_v)
+            store(h, b)
+
+        def finish_last():
+            o_v = result_tile(LAST)
+            dst = unit_out(LAST, 1).rearrange("h (p e) d -> e p h d", e=2)
+            for e, queue in ((0, nc.sync), (1, nc.scalar)):
+                acc_v = sums[(LAST, 1, e)][:].rearrange("p (e h d) -> p e h d", e=2, h=2)
+                nc.scalar.copy(out=o_v[:, 2 + e], in_=acc_v[:, e])
+                queue.dma_start(out=dst[e], in_=o_v[:, 2 + e])
 
         for h in (0, 2, 1):
-            head_half(h, 0)
-            head_half(h, 1)
-        multiply(2, (0,))
-        transposes(3, (0, 1))
-        evacuate(3, (0, 1), (1,))
+            for r in range(2):
+                transposes(h, r)
+                quantise_rows(h, r)
+        multiply(2, 0)
+        transposes(3, 0)
         build_tables()
-        quantise(3, ((0, 512),))
-        multiply(2, (1,))
-        transposes(3, (2, 3))
-        evacuate(3, (2, 3), ())
+        multiply(2, 1, (0,))
+        transposes(3, 1)
         products(2, 0)
-        quantise(3, ((512, 1024),))
-        transposes(4, ALL)
-        evacuate(4, ALL, ())
+        quantise(3)
+        transposes(4, 0)
+        permute(5, 0)
+        multiply(2, 1, (1,))
+        transposes(4, 1)
+        permute(5, 1)
         products(2, 1)
-        combine(2)
+        combine(2, WHOLE, nc.vector)
         store(2, 0)
         store(2, 1)
-        multiply(3, (0,))
-        transposes(5, ALL)
-        evacuate(5, (0, 1), ())
-        permute(6)
-        evacuate(5, (2, 3), ())
-        quantise(4, WHOLE)
-        multiply(3, (1,))
-        transposes(6, (0, 1))
-        evacuate(6, (0, 1), ())
-        permute(7)
+        multiply(3, 0)
+        transposes(5, 0)
+        permute(6, 0)
+        transposes(5, 1)
+        permute(6, 1)
+        quantise(4)
+        multiply(3, 1)
+        transposes(6, 0)
+        permute(7, 0)
         finish(3)
-        quantise(5, WHOLE)
-        multiply(4, (0,))
-        transposes(6, (2, 3))
-        evacuate(6, (2, 3), ())
-        multiply(4, (1,))
-        for m in range(5, 14):
-            if m + 2 <= 13:
-                transposes(m + 2, (0, 1))
-                evacuate(m + 2, (0, 1), ())
-            if m + 3 <= 13:
-                permute(m + 3)
-            products(m - 1, 0)
-            if m - 1 >= FIRST_V_UNIT:
-                store(m - 1, 0)
-            products(m - 1, 1)
-            if m == 12:
-                quantise(13, WHOLE)
-            combine(m - 1)
-            if m - 1 < FIRST_V_UNIT:
-                store(m - 1, 0)
-            store(m - 1, 1)
-            if m + 1 <= 12:
-                quantise(m + 1, WHOLE)
-            multiply(m, (0,))
-            if m + 2 <= 13:
-                transposes(m + 2, (2, 3))
-                evacuate(m + 2, (2, 3), ())
-            multiply(m, (1,))
-        products(13, 0)
-        store(13, 0)
-        products(13, 1)
-        store(13, 1)
+        quantise(5)
+        multiply(4, 0)
+        transposes(6, 1)
+        permute(7, 1)
+        multiply(4, 1)
+        for m in range(5, UNITS):
+            for b in range(2):
+                if m + 2 < UNITS:
+                    transposes(m + 2, b)
+                if m + 3 < UNITS:
+                    permute(m + 3, b)
+                if b == 0:
+                    if m < 11:
+                        finish(m - 1)
+                        quantise(m + 1)
+                    elif m < 13:
+                        finish_halves(m - 1, m + 1)
+                    else:
+                        finish_v(12, 0)
+                        finish_v(12, 1)
+                multiply(m, b)
+        finish_v(LAST, 0)
+        finish_last()

@@ -114,8 +114,6 @@ def tile_mistralattention_kernel(
         terms = {}
 
         def permute(h, i):
-            if i == 1 and h % 2 == 0:
-                return
             t = perm_pool.tile([P, 1024], F32, name="perm_t")
             permuted[(h, i)] = t
             words = src[h][:].bitcast(F32).rearrange("p (r g q u) -> p r g u q", r=2, g=4, u=2)
@@ -279,10 +277,8 @@ def tile_mistralattention_kernel(
         products(2, 0)
         quantise(3)
         transposes(4, 0)
-        permute(5, 0)
         multiply(2, 1, (1,))
         transposes(4, 1)
-        permute(5, 1)
         products(2, 1)
         combine(2, WHOLE, nc.vector)
         store(2, 0)
@@ -291,7 +287,6 @@ def tile_mistralattention_kernel(
         transposes(5, 0)
         permute(6, 0)
         transposes(5, 1)
-        permute(6, 1)
         quantise(4)
         multiply(3, 1)
         transposes(6, 0)
@@ -300,14 +295,13 @@ def tile_mistralattention_kernel(
         quantise(5)
         multiply(4, 0)
         transposes(6, 1)
-        permute(7, 1)
         multiply(4, 1)
         for m in range(5, UNITS):
             for b in range(2):
                 if m + 2 < UNITS:
                     transposes(m + 2, b)
-                if m + 3 < UNITS:
-                    permute(m + 3, b)
+                if b == 0 and m + 3 < UNITS:
+                    permute(m + 3, 0)
                 if b == 0:
                     if m < 11:
                         finish(m - 1)

@@ -15,11 +15,10 @@ ADD = mybir.AluOpType.add
 
 P = 128
 UNITS = 14
-LAST = 13
 LOAD_ORDER = (0, 2, 1, 3, 4, 5, 6, 7, 8, 9, 10, 11, 12, 13)
 SPLIT = (0, 1, 2, 3)
-FIRST_PERMUTED = 5
 FIRST_V_UNIT = 12
+VECTOR_ADDS = (2, 11)
 
 
 def tile_mistralattention_kernel(
@@ -29,7 +28,7 @@ def tile_mistralattention_kernel(
     with ExitStack() as ctx:
         src_pool = ctx.enter_context(tc.tile_pool(name="src", bufs=1))
         const_pool = ctx.enter_context(tc.tile_pool(name="const", bufs=1))
-        perm_pool = ctx.enter_context(tc.tile_pool(name="perm", bufs=6))
+        perm_pool = ctx.enter_context(tc.tile_pool(name="perm", bufs=3))
         grp_pool = ctx.enter_context(tc.tile_pool(name="grp", bufs=3))
         xq_pool = ctx.enter_context(tc.tile_pool(name="xq", bufs=1))
         wq_pool = ctx.enter_context(tc.tile_pool(name="wq", bufs=3))
@@ -114,20 +113,20 @@ def tile_mistralattention_kernel(
         terms = {}
 
         def permute(h, i):
-            t = perm_pool.tile([P, 1024], F32, name="perm_t")
+            if i == 1 and h % 2 == 0:
+                return
+            n = 2 - i
+            t = perm_pool.tile([P, 512 * n], F32, name="perm%d" % i)
             permuted[(h, i)] = t
-            words = src[h][:].bitcast(F32).rearrange("p (r g q u) -> p r g u q", r=2, g=4, u=2)
-            source = words[:, :, 2 * i : 2 * i + 2]
-            target = t[:].rearrange("p (r g u q) -> p r g u q", r=2, g=2, u=2)
-            if i == 0:
-                nc.scalar.copy(out=target, in_=source)
-            else:
-                nc.vector.tensor_copy(out=target, in_=source)
+            source = src[h][:].bitcast(F32).rearrange("p (r g q u) -> p r g u q", r=2, g=4, u=2)
+            target = t[:].rearrange("p (r g u q) -> p r g u q", r=2, g=n, u=2)
+            nc.scalar.copy(out=target, in_=source[:, :, 2 * i : 2 * i + n])
 
         def words(h, g, u, r):
-            if (h, g // 2) in permuted:
-                col = 512 * r + 256 * (g % 2) + 128 * u
-                return permuted[(h, g // 2)][:, col : col + 128]
+            if (h, g // 2) in permuted and g < 3:
+                i = g // 2
+                col = 256 * (2 - i) * r + 256 * (g % 2) + 128 * u
+                return permuted[(h, i)][:, col : col + 128]
             if h in SPLIT:
                 col = 256 * g
                 return src[(h, r)][:].bitcast(F32)[:, col + u : col + 256 : 2]
@@ -181,13 +180,10 @@ def tile_mistralattention_kernel(
             else:
                 quantise(h, tuple((256 * g + 128 * r, 256 * g + 128 * r + 128) for g in range(4)))
 
-        def multiply(h, b, es=(0, 1)):
-            for e in es:
-                if e == 0 or (h, b) == (LAST, 1):
-                    sums[(h, b, e)] = acc_pool.tile([P, 512], F32, name="acc")
-                else:
-                    sums[(h, b, e)] = sums[(h, b, 0)]
-                acc = sums[(h, b, e)]
+        def multiply(h, b):
+            acc = acc_pool.tile([P, 512], F32, name="acc")
+            sums[(h, b)] = acc
+            for e in range(2):
                 for g in range(4):
                     xs = slice(512 * e + 128 * g, 512 * e + 128 * g + 128)
                     ws = slice(256 * g, 256 * g + 256)
@@ -210,7 +206,7 @@ def tile_mistralattention_kernel(
             if h not in terms:
                 terms[h] = term_pool.tile([P, 2048], F32, name="t_t")
             t_v = terms[h][:].rearrange("p (f b q c j) -> p f b q c j", f=2, b=2, q=4, c=2)
-            acc_v = sums[(h, b, 0)][:].rearrange("p (q f j) -> p q f j", q=4, f=2)
+            acc_v = sums[(h, b)][:].rearrange("p (q f j) -> p q f j", q=4, f=2)
             for f in range(2):
                 nc.vector.tensor_tensor(
                     out=t_v[:, f, b],
@@ -219,11 +215,10 @@ def tile_mistralattention_kernel(
                     op=MULT,
                 )
 
-        def combine(h, ts, eng):
+        def combine(h):
             t_v = terms[h][:].rearrange("p (f t h d) -> p f t h d", f=2, t=4, h=2)
-            eng.tensor_tensor(
-                out=result_tile(h)[:, ts], in0=t_v[:, 0, ts], in1=t_v[:, 1, ts], op=ADD
-            )
+            eng = nc.vector if h in VECTOR_ADDS else nc.gpsimd
+            eng.tensor_tensor(out=result_tile(h), in0=t_v[:, 0], in1=t_v[:, 1], op=ADD)
 
         def store(h, b):
             o_b = results[h][:].rearrange("p (h b x) -> p h b x", h=2, b=2)
@@ -232,38 +227,22 @@ def tile_mistralattention_kernel(
                 out=unit_out(h, b).rearrange("h (p e) d -> p h (e d)", e=2), in_=o_b[:, :, b, :]
             )
 
-        WHOLE = slice(0, 4)
-        HALF = (slice(0, 2), slice(2, 4))
-
-        def finish(h):
+        def finish(h, q=None):
             products(h, 0)
             products(h, 1)
-            combine(h, WHOLE, nc.gpsimd)
+            if q is not None:
+                quantise(q)
+            combine(h)
             store(h, 0)
             store(h, 1)
 
-        def finish_halves(h, q):
-            products(h, 0)
-            combine(h, HALF[0], nc.gpsimd)
-            store(h, 0)
-            products(h, 1)
-            quantise(q)
-            combine(h, HALF[1], nc.vector)
-            store(h, 1)
-
-        def finish_v(h, b):
-            o_v = result_tile(h)
-            acc_v = sums[(h, b, 0)][:].rearrange("p (e h d) -> p e h d", e=2, h=2)
-            nc.scalar.copy(out=o_v[:, HALF[b]], in_=acc_v)
-            store(h, b)
-
-        def finish_last():
-            o_v = result_tile(LAST)
-            dst = unit_out(LAST, 1).rearrange("h (p e) d -> e p h d", e=2)
-            for e, queue in ((0, nc.sync), (1, nc.scalar)):
-                acc_v = sums[(LAST, 1, e)][:].rearrange("p (e h d) -> p e h d", e=2, h=2)
-                nc.scalar.copy(out=o_v[:, 2 + e], in_=acc_v[:, e])
-                queue.dma_start(out=dst[e], in_=o_v[:, 2 + e])
+        def finish_v(h):
+            for b in range(2):
+                nc.scalar.copy(
+                    out=result_tile(h)[:, 2 * b : 2 * b + 2],
+                    in_=sums[(h, b)][:].rearrange("p (e h d) -> p e h d", e=2, h=2),
+                )
+                store(h, b)
 
         for h in (0, 2, 1):
             for r in range(2):
@@ -272,21 +251,21 @@ def tile_mistralattention_kernel(
         multiply(2, 0)
         transposes(3, 0)
         build_tables()
-        multiply(2, 1, (0,))
+        multiply(2, 1)
         transposes(3, 1)
         products(2, 0)
         quantise(3)
         transposes(4, 0)
-        multiply(2, 1, (1,))
         transposes(4, 1)
         products(2, 1)
-        combine(2, WHOLE, nc.vector)
+        combine(2)
         store(2, 0)
         store(2, 1)
         multiply(3, 0)
         transposes(5, 0)
         permute(6, 0)
         transposes(5, 1)
+        permute(6, 1)
         quantise(4)
         multiply(3, 1)
         transposes(6, 0)
@@ -295,22 +274,21 @@ def tile_mistralattention_kernel(
         quantise(5)
         multiply(4, 0)
         transposes(6, 1)
+        permute(7, 1)
         multiply(4, 1)
         for m in range(5, UNITS):
             for b in range(2):
                 if m + 2 < UNITS:
                     transposes(m + 2, b)
-                if b == 0 and m + 3 < UNITS:
-                    permute(m + 3, 0)
+                if m + 3 < UNITS:
+                    permute(m + 3, b)
                 if b == 0:
-                    if m < 11:
+                    if m < 12:
                         finish(m - 1)
                         quantise(m + 1)
-                    elif m < 13:
-                        finish_halves(m - 1, m + 1)
+                    elif m == 12:
+                        finish(11, 13)
                     else:
-                        finish_v(12, 0)
-                        finish_v(12, 1)
+                        finish_v(12)
                 multiply(m, b)
-        finish_v(LAST, 0)
-        finish_last()
+        finish_v(13)

from contextlib import ExitStack

import concourse.mybir as mybir
from concourse.masks import make_identity

FLOPS = 2 * 512 * 3072 * 2048

BF16 = mybir.dt.bfloat16
F32 = mybir.dt.float32
U32 = mybir.dt.uint32
U8 = mybir.dt.uint8
FP8X4 = mybir.dt.float8_e4m3fn_x4
MULT = mybir.AluOpType.mult
ADD = mybir.AluOpType.add

P = 128
UNITS = 14
LOAD_ORDER = (0, 2, 1, 3, 4, 5, 6, 7, 8, 9, 10, 11, 12, 13)
SPLIT = (0, 1, 2, 3)
FIRST_V_UNIT = 12
VECTOR_ADDS = (2, 11)


def tile_mistralattention_kernel(
    tc, hidden_states, cos, sin, q_w, k_w, v_w, out_0, out_1, out_2
):
    nc = tc.nc
    with ExitStack() as ctx:
        src_pool = ctx.enter_context(tc.tile_pool(name="src", bufs=1))
        const_pool = ctx.enter_context(tc.tile_pool(name="const", bufs=1))
        perm_pool = ctx.enter_context(tc.tile_pool(name="perm", bufs=3))
        grp_pool = ctx.enter_context(tc.tile_pool(name="grp", bufs=3))
        xq_pool = ctx.enter_context(tc.tile_pool(name="xq", bufs=1))
        wq_pool = ctx.enter_context(tc.tile_pool(name="wq", bufs=3))
        term_pool = ctx.enter_context(tc.tile_pool(name="term", bufs=2))
        out_pool = ctx.enter_context(tc.tile_pool(name="outp", bufs=5))
        tp_pool = ctx.enter_context(tc.psum_pool(name="tp", bufs=4))
        acc_pool = ctx.enter_context(tc.psum_pool(name="acc", bufs=4))
        ctx.enter_context(tc.manual_schedule())

        def unit_rows(h):
            if h < 2:
                return hidden_states[h].rearrange("(p e) k -> p e k", e=2)
            w = h - 2
            if w < 8:
                rows = q_w[256 * w : 256 * w + 256, :]
            elif w < 10:
                rows = k_w[256 * (w - 8) : 256 * (w - 8) + 256, :]
            else:
                rows = v_w[256 * (w - 10) : 256 * (w - 10) + 256, :]
            return rows.rearrange("(r p) k -> p r k", p=P)

        def unit_out(h, b):
            w = h - 2
            if w < 8:
                return out_0[b, 2 * w : 2 * w + 2]
            if w < 10:
                return out_1[b, 2 * (w - 8) : 2 * (w - 8) + 2]
            return out_2[b, 2 * (w - 10) : 2 * (w - 10) + 2]

        ident = const_pool.tile([P, P], F32, name="ident")
        make_identity(nc, ident[:])
        cos_sb = const_pool.tile([P, 512], BF16, name="cos_sb")
        sin_sb = const_pool.tile([P, 512], BF16, name="sin_sb")

        src = {}
        for h in LOAD_ORDER:
            rows = unit_rows(h)
            if h in SPLIT:
                for r in range(2):
                    s_t = src_pool.tile([P, 2048], BF16, name="src%d_%d" % (h, r))
                    src[(h, r)] = s_t
                    nc.sync.dma_start(out=s_t[:], in_=rows[:, r, :])
            else:
                s_t = src_pool.tile([P, 4096], BF16, name="src%d" % h)
                src[h] = s_t
                nc.sync.dma_start(out=s_t[:].rearrange("p (r k) -> p r k", r=2), in_=rows)
            if h == 3:
                for table, source in ((cos_sb, cos), (sin_sb, sin)):
                    nc.sync.dma_start(
                        out=table[:].rearrange("p (b x) -> p b x", b=2),
                        in_=source.rearrange("b (p e) d -> p b (e d)", e=2),
                    )

        tab = const_pool.tile([P, 2048], F32, name="tab")
        tab_w = tab[:].rearrange("p (f t h c j) -> p f t h c j", f=2, t=4, h=2, c=2)
        tab_r = tab[:].rearrange("p (f b q c j) -> p f b q c j", f=2, b=2, q=4, c=2)
        cos_v = cos_sb[:].rearrange("p (t f j) -> p t f j", t=4, f=2)
        sin_v = sin_sb[:].rearrange("p (t f j) -> p t f j", t=4, f=2)

        def build_tables():
            for eng, f, c, view, half, sign in (
                (nc.vector, 0, 0, cos_v, 0, 1.0),
                (nc.gpsimd, 0, 1, sin_v, 1, 1.0),
                (nc.vector, 1, 1, cos_v, 1, 1.0),
                (nc.gpsimd, 1, 0, sin_v, 0, -1.0),
            ):
                eng.tensor_scalar(
                    out=tab_w[:, f, :, :, c, :],
                    in0=view[:, :, half, :].unsqueeze(2).to_broadcast([P, 4, 2, 64]),
                    scalar1=sign,
                    scalar2=0.0,
                    op0=MULT,
                    op1=ADD,
                )

        permuted = {}
        grouped = {}
        codes = {}
        planes = {}
        sums = {}
        results = {}
        terms = {}

        def permute(h, i):
            if i == 1 and h % 2 == 0:
                return
            n = 2 - i
            t = perm_pool.tile([P, 512 * n], F32, name="perm%d" % i)
            permuted[(h, i)] = t
            source = src[h][:].bitcast(F32).rearrange("p (r g q u) -> p r g u q", r=2, g=4, u=2)
            target = t[:].rearrange("p (r g u q) -> p r g u q", r=2, g=n, u=2)
            nc.scalar.copy(out=target, in_=source[:, :, 2 * i : 2 * i + n])

        def words(h, g, u, r):
            if (h, g // 2) in permuted and g < 3:
                i = g // 2
                col = 256 * (2 - i) * r + 256 * (g % 2) + 128 * u
                return permuted[(h, i)][:, col : col + 128]
            if h in SPLIT:
                col = 256 * g
                return src[(h, r)][:].bitcast(F32)[:, col + u : col + 256 : 2]
            col = 1024 * r + 256 * g
            return src[h][:].bitcast(F32)[:, col + u : col + 256 : 2]

        def transposes(h, i):
            if h not in grouped:
                grouped[h] = grp_pool.tile([P, 4096], BF16, name="grp", align_bytes=64)
            g_f = grouped[h][:].bitcast(F32)
            for q in range(2):
                bank = tp_pool.tile([P, 512], F32, name="bank")
                for y in range(2):
                    for u in range(2):
                        if h in SPLIT:
                            place, source = 256 * y + 128 * u, words(h, 2 * q + y, u, i)
                        else:
                            place, source = 256 * u + 128 * y, words(h, 2 * i + q, u, y)
                        nc.tensor.transpose(bank[:, place : place + 128], source, ident[:])
                if h < 2:
                    col = 1024 * i + 512 * q
                    dst = g_f[:, col : col + 512].rearrange("p (y o u) -> p y o u", y=2, u=2)
                elif h in SPLIT:
                    dst = g_f.rearrange("p (g r o u) -> p r g o u", g=4, r=2, u=2)
                    dst = dst[:, i, 2 * q : 2 * q + 2]
                else:
                    col = 512 * (2 * i + q)
                    dst = g_f[:, col : col + 512].rearrange("p (o u) -> p o u", u=2)
                if h in SPLIT:
                    view = bank[:].rearrange("p (y u o) -> p y o u", y=2, u=2)
                else:
                    view = bank[:].rearrange("p (u o) -> p o u", u=2)
                nc.scalar.copy(out=dst, in_=view)

        def quantise(h, parts=((0, 1024),)):
            if h not in codes:
                pool = xq_pool if h < 2 else wq_pool
                tag = "x%d" % h if h < 2 else "w"
                codes[h] = pool.tile([P, 1024], U32, name="codes_" + tag, align_bytes=64)
                planes[h] = pool.tile([P, 1024], U8, name="plane_" + tag, align_bytes=64)
            for lo, hi in parts:
                nc.vector.quantize_mx(
                    out=codes[h][:, lo:hi].bitcast(FP8X4),
                    scales=planes[h][:, lo:hi],
                    in_=grouped[h][:, 4 * lo : 4 * hi],
                )

        def quantise_rows(h, r):
            if h < 2:
                quantise(h, ((512 * r, 512 * r + 512),))
            else:
                quantise(h, tuple((256 * g + 128 * r, 256 * g + 128 * r + 128) for g in range(4)))

        def multiply(h, b):
            acc = acc_pool.tile([P, 512], F32, name="acc")
            sums[(h, b)] = acc
            for e in range(2):
                for g in range(4):
                    xs = slice(512 * e + 128 * g, 512 * e + 128 * g + 128)
                    ws = slice(256 * g, 256 * g + 256)
                    nc.tensor.matmul_mx(
                        out=acc[:, 256 * e : 256 * e + 256],
                        lhsT=codes[b][:, xs].bitcast(FP8X4),
                        lhsT_scale=planes[b][:, xs],
                        rhs=codes[h][:, ws].bitcast(FP8X4),
                        rhs_scale=planes[h][:, ws],
                        start=(g == 0),
                        stop=(g == 3),
                    )

        def result_tile(h):
            if h not in results:
                results[h] = out_pool.tile([P, 1024], F32, name="o_t")
            return results[h][:].rearrange("p (h t d) -> p t h d", h=2, t=4)

        def products(h, b):
            if h not in terms:
                terms[h] = term_pool.tile([P, 2048], F32, name="t_t")
            t_v = terms[h][:].rearrange("p (f b q c j) -> p f b q c j", f=2, b=2, q=4, c=2)
            acc_v = sums[(h, b)][:].rearrange("p (q f j) -> p q f j", q=4, f=2)
            for f in range(2):
                nc.vector.tensor_tensor(
                    out=t_v[:, f, b],
                    in0=acc_v[:, :, f : f + 1, :].to_broadcast([P, 4, 2, 64]),
                    in1=tab_r[:, f, b],
                    op=MULT,
                )

        def combine(h):
            t_v = terms[h][:].rearrange("p (f t h d) -> p f t h d", f=2, t=4, h=2)
            eng = nc.vector if h in VECTOR_ADDS else nc.gpsimd
            eng.tensor_tensor(out=result_tile(h), in0=t_v[:, 0], in1=t_v[:, 1], op=ADD)

        def store(h, b):
            o_b = results[h][:].rearrange("p (h b x) -> p h b x", h=2, b=2)
            queue = nc.scalar if h >= FIRST_V_UNIT else nc.sync
            queue.dma_start(
                out=unit_out(h, b).rearrange("h (p e) d -> p h (e d)", e=2), in_=o_b[:, :, b, :]
            )

        def finish(h, q=None):
            products(h, 0)
            products(h, 1)
            if q is not None:
                quantise(q)
            combine(h)
            store(h, 0)
            store(h, 1)

        def finish_v(h):
            for b in range(2):
                nc.scalar.copy(
                    out=result_tile(h)[:, 2 * b : 2 * b + 2],
                    in_=sums[(h, b)][:].rearrange("p (e h d) -> p e h d", e=2, h=2),
                )
                store(h, b)

        for h in (0, 2, 1):
            for r in range(2):
                transposes(h, r)
                quantise_rows(h, r)
        multiply(2, 0)
        transposes(3, 0)
        build_tables()
        multiply(2, 1)
        transposes(3, 1)
        products(2, 0)
        quantise(3)
        transposes(4, 0)
        transposes(4, 1)
        products(2, 1)
        combine(2)
        store(2, 0)
        store(2, 1)
        multiply(3, 0)
        transposes(5, 0)
        permute(6, 0)
        transposes(5, 1)
        permute(6, 1)
        quantise(4)
        multiply(3, 1)
        transposes(6, 0)
        permute(7, 0)
        finish(3)
        quantise(5)
        multiply(4, 0)
        transposes(6, 1)
        permute(7, 1)
        multiply(4, 1)
        for m in range(5, UNITS):
            for b in range(2):
                if m + 2 < UNITS:
                    transposes(m + 2, b)
                if m + 3 < UNITS:
                    permute(m + 3, b)
                if b == 0:
                    if m < 12:
                        finish(m - 1)
                        quantise(m + 1)
                    elif m == 12:
                        finish(11, 13)
                    else:
                        finish_v(12)
                multiply(m, b)
        finish_v(13)
